import numpy as np
import ml_dtypes


def mxq(x, axis, fmt="e4m3"):
    dtype, down = {"e4m3": (ml_dtypes.float8_e4m3fn, 7), "e5m2": (ml_dtypes.float8_e5m2, 14)}[fmt]
    v = np.moveaxis(np.asarray(x, np.float32).astype(ml_dtypes.bfloat16).astype(np.float64), axis, -1)
    blocks = v.reshape(v.shape[:-1] + (-1, 32))
    amax = np.abs(blocks).max(-1, keepdims=True)
    byte = np.maximum(np.where(amax > 0, np.frexp(amax)[1] - 1 + 127, 0) - down, 1)
    scale = np.exp2(byte - 127.0)
    codes = (blocks / scale).astype(np.float32).astype(dtype).astype(np.float64)
    return np.moveaxis((codes * scale).reshape(v.shape), -1, axis)


WIDE = False


def mx_kscale(k):
    if not WIDE:
        return np.ones(k)
    levels = np.array([10, -10, 5, -5, 0])
    a = np.random.permutation(np.resize(levels, k // 512 * 4)).reshape(k // 512, 4)
    idx = np.arange(k)
    return np.exp2(a[idx // 512, idx % 128 // 32])


BF16 = ml_dtypes.bfloat16


def bf(x):
    return np.asarray(x, np.float32).astype(BF16)


def f64(x):
    return np.asarray(x).astype(np.float64)


E2M1 = np.array([0.0, 0.5, 1.0, 1.5, 2.0, 3.0, 4.0, 6.0, -0.0, -0.5, -1.0, -1.5, -2.0, -3.0, -4.0, -6.0])


def pack_weight(w, fmt):
    k, n = w.shape
    w = f64(bf(w)).reshape(k // 32, 32, n)
    amax = np.abs(w).max(1)
    if fmt == "e4m3":
        byte = np.frexp(amax)[1] - 1 + 127 - 7
    else:
        mant, ex = np.frexp(amax / 6.0)
        byte = np.where(mant > 0.5, ex, ex - 1) + 127
    byte = np.clip(np.where(amax > 0, byte, 1), 1, 254)
    scaled = (w * np.exp2(127.0 - byte)[:, None, :]).reshape(k, n).astype(np.float32)
    by_word = np.ascontiguousarray(scaled.reshape(k // 512, 128, 4, n).transpose(0, 1, 3, 2))
    if fmt == "e4m3":
        words = by_word.astype(ml_dtypes.float8_e4m3fn).view(np.uint8)
    else:
        c = by_word.astype(ml_dtypes.float4_e2m1fn).view(np.uint8) & 0xF
        words = c[..., 0::2] | (c[..., 1::2] << 4)
    return np.ascontiguousarray(words), np.ascontiguousarray(byte.astype(np.uint8).reshape(k // 512, 16, n))


def unpack_weight(words, scales, fmt):
    g, p, n, _ = words.shape
    if fmt == "e4m3":
        vals = np.ascontiguousarray(words).view(ml_dtypes.float8_e4m3fn).astype(np.float64)
    else:
        nib = np.empty((g, p, n, 4), np.uint8)
        nib[..., 0::2] = words & 0xF
        nib[..., 1::2] = words >> 4
        vals = E2M1[nib]
    vals = vals * np.repeat(np.exp2(scales.astype(np.float64) - 127.0), 8, axis=1)[..., None]
    return vals.transpose(0, 1, 3, 2).reshape(g * 512, n)


N, IN_DIM, HID, OUT_DIM = 1024, 1024, 512, 256


def setup_inputs():
    s = mx_kscale(IN_DIM)
    X = bf(np.random.standard_normal((N, IN_DIM)) * s)
    A = bf(np.random.uniform(0.0, 1.0, (N, N)) * 0.5 / np.sqrt(N))
    W_in_words, W_in_scales = pack_weight(np.random.standard_normal((IN_DIM, HID)) / np.sqrt(IN_DIM) / s[:, None], "e4m3")
    b_in = bf(np.random.standard_normal(HID) * 0.1)
    eps0 = bf(np.random.uniform(0.2, 0.4, (1,)))
    return {"X": X,
            "A": A,
            "W_in_words": W_in_words,
            "W_in_scales": W_in_scales,
            "b_in": b_in,
            "eps0": eps0}


def reference(X, A, W_in_words, W_in_scales, b_in, eps0):
    h = (mxq(f64(X), 1, "e4m3") @ unpack_weight(W_in_words, W_in_scales, "e4m3")) + f64(b_in)
    return (mxq(f64(A), 1, "e4m3") @ mxq(h, 0, "e4m3")) + (1.0 + f64(eps0)) * h

@@ -1,0 +1,183 @@
+from contextlib import ExitStack
+
+import concourse.mybir as mybir
+from concourse.masks import make_identity
+
+F32 = mybir.dt.float32
+BF16 = mybir.dt.bfloat16
+I32 = mybir.dt.int32
+U32 = mybir.dt.uint32
+U8 = mybir.dt.uint8
+FP8X4 = mybir.dt.float8_e4m3fn_x4
+ADD = mybir.AluOpType.add
+MULT = mybir.AluOpType.mult
+
+P = 128
+PACK = 4
+K_PASS = P * PACK
+NODES = 1024
+FEATURES = 1024
+HIDDEN = 512
+PASSES = 2
+PAIRS = NODES // (2 * P)
+AHEAD = 2
+WORDS = K_PASS // 2
+
+FLOPS = 2 * NODES * FEATURES * HIDDEN + 2 * NODES * NODES * HIDDEN
+
+
+def tile_gin_pa_kernel(tc, X, A, W_in_words, W_in_scales, b_in, eps0, out):
+    nc = tc.nc
+    x_pairs = X.rearrange("(i p e) k -> i p e k", p=P, e=2)
+    a_pairs = A.rearrange("(i p e) k -> i p e k", p=P, e=2)
+    out_pairs = out.rearrange("(i p e) f -> i p e f", p=P, e=2)
+
+    with ExitStack() as ctx:
+        keep = ctx.enter_context(tc.tile_pool(name="keep", bufs=1))
+        turned_banks = ctx.enter_context(tc.psum_pool(name="turned_banks", bufs=4))
+        sum_banks = ctx.enter_context(tc.psum_pool(name="sum_banks", bufs=4))
+        ctx.enter_context(tc.manual_schedule())
+
+        x_rows = [keep.tile([P, 2, FEATURES], BF16, name="x_rows%d" % i) for i in range(PAIRS)]
+        a_rows = [keep.tile([P, 2, NODES], BF16, name="a_rows%d" % i) for i in range(PAIRS)]
+        w_codes = keep.tile([P, PASSES, PACK * HIDDEN], U8, name="w_codes", align_bytes=64)
+        w_scales = keep.tile([P, PASSES, HIDDEN], U8, name="w_scales", align_bytes=64)
+        bias = keep.tile([P, HIDDEN], BF16, name="bias")
+        eps = keep.tile([P, 1], BF16, name="eps")
+        one_plus_eps = keep.tile([P, 1], F32, name="one_plus_eps")
+        identity = keep.tile([P, P], F32, name="identity")
+        h = [keep.tile([P, PACK, HIDDEN], F32, name="h%d" % g) for g in range(PASSES)]
+        h_grouped = [
+            keep.tile([P, HIDDEN, PACK], BF16, name="h_grouped%d" % g, align_bytes=64)
+            for g in range(PASSES)
+        ]
+        h_codes = [keep.tile([P, HIDDEN], U32, name="h_codes%d" % g, align_bytes=64) for g in range(PASSES)]
+        h_scales = [keep.tile([P, HIDDEN], U8, name="h_scales%d" % g, align_bytes=64) for g in range(PASSES)]
+        result = [keep.tile([P, 2, HIDDEN], F32, name="result%d" % i) for i in range(PAIRS)]
+
+        def quantised_pair(name):
+            return {
+                "grouped": keep.tile([P, 2, PASSES, P, PACK], BF16, name=name + "_grouped", align_bytes=64),
+                "codes": keep.tile([P, 2, PASSES, P], U32, name=name + "_codes", align_bytes=64),
+                "scales": keep.tile([P, 2, PASSES, P], U8, name=name + "_scales", align_bytes=64),
+            }
+
+        x_mx = [quantised_pair("x%d" % i) for i in range(PAIRS)]
+        a_mx = [quantised_pair("a%d" % i) for i in range(PAIRS)]
+
+        nc.vector.memset(w_scales[:].rearrange("p g n -> p (g n)").bitcast(I32), 0)
+        make_identity(nc, identity[:])
+        nc.gpsimd.dma_start(out=bias[:], in_=b_in.partition_broadcast(P))
+        nc.gpsimd.dma_start(out=eps[:], in_=eps0.partition_broadcast(P))
+
+        nc.sync.dma_start(out=x_rows[0][:], in_=x_pairs[0])
+        nc.sync.dma_start(out=x_rows[1][:], in_=x_pairs[1])
+        scale_rows = W_in_scales.rearrange("g (q r) n -> r q g n", r=4)
+        for r in range(4):
+            nc.sync.dma_start(out=w_scales[r:P:32].bitcast(I32), in_=scale_rows[r].bitcast(I32))
+        nc.sync.dma_start(
+            out=w_codes[:].bitcast(I32),
+            in_=W_in_words.rearrange("g p n t -> p g (n t)").bitcast(I32),
+        )
+        for i in range(AHEAD, PAIRS):
+            nc.sync.dma_start(out=x_rows[i][:], in_=x_pairs[i])
+        for i in range(PAIRS):
+            nc.sync.dma_start(out=a_rows[i][:], in_=a_pairs[i])
+
+        nc.vector.tensor_scalar_add(out=one_plus_eps[:], in0=eps[:], scalar1=1.0)
+
+        def turn_and_quantise(rows, mx, interleaved):
+            for e in range(2):
+                words = rows[:, e, :].bitcast(F32)
+                turned = turned_banks.tile([P, PASSES, 2, P], F32)
+                for g in range(PASSES):
+                    for u in range(2):
+                        if interleaved:
+                            columns = words[:, WORDS * g + u : WORDS * (g + 1) : 2]
+                        else:
+                            columns = words[:, WORDS * g + P * u : WORDS * g + P * (u + 1)]
+                        nc.tensor.transpose(turned[:, g, u, :], columns, identity[:])
+                nc.scalar.copy(
+                    out=mx["grouped"][:, e].bitcast(F32),
+                    in_=turned[:].rearrange("p g u n -> p g n u"),
+                )
+            nc.vector.quantize_mx(
+                out=mx["codes"][:].rearrange("p e g n -> p (e g n)").bitcast(FP8X4),
+                scales=mx["scales"][:].rearrange("p e g n -> p (e g n)"),
+                in_=mx["grouped"][:].rearrange("p e g n t -> p (e g n t)"),
+            )
+
+        def multiply(mx, e, moving_codes, moving_scales):
+            sums = sum_banks.tile([P, HIDDEN], F32)
+            for g in range(PASSES):
+                nc.tensor.matmul_mx(
+                    out=sums[:],
+                    lhsT=mx["codes"][:, e, g, :].bitcast(FP8X4),
+                    lhsT_scale=mx["scales"][:, e, g, :],
+                    rhs=moving_codes[g],
+                    rhs_scale=moving_scales[g],
+                    start=(g == 0),
+                    stop=(g == PASSES - 1),
+                )
+            return sums
+
+        def project(i):
+            for e in range(2):
+                sums = multiply(
+                    x_mx[i],
+                    e,
+                    [w_codes[:, g, :].bitcast(FP8X4) for g in range(PASSES)],
+                    [w_scales[:, g, :] for g in range(PASSES)],
+                )
+                j = 2 * i + e
+                nc.vector.tensor_tensor(out=h[j // PACK][:, j % PACK, :], in0=sums[:], in1=bias[:], op=ADD)
+
+        def quantise_h(g):
+            half = HIDDEN // 2
+            for copy, columns in ((nc.vector.tensor_copy, slice(0, half)), (nc.scalar.copy, slice(half, HIDDEN))):
+                copy(
+                    out=h_grouped[g][:, columns, :].rearrange("p (c i) t -> p c t i", i=4),
+                    in_=h[g][:, :, columns].rearrange("p t (c i) -> p c t i", i=4),
+                )
+            nc.vector.quantize_mx(
+                out=h_codes[g][:].bitcast(FP8X4),
+                scales=h_scales[g][:],
+                in_=h_grouped[g][:].rearrange("p f t -> p (f t)"),
+            )
+
+        def aggregate(i):
+            for e in range(2):
+                sums = multiply(
+                    a_mx[i],
+                    e,
+                    [h_codes[g][:].bitcast(FP8X4) for g in range(PASSES)],
+                    [h_scales[g][:] for g in range(PASSES)],
+                )
+                j = 2 * i + e
+                nc.vector.scalar_tensor_tensor(
+                    out=result[i][:, e, :],
+                    in0=h[j // PACK][:, j % PACK, :],
+                    scalar=one_plus_eps[:, 0:1],
+                    in1=sums[:],
+                    op0=MULT,
+                    op1=ADD,
+                )
+                nc.sync.dma_start(out=out_pairs[i][:, e, :], in_=result[i][:, e, :])
+
+        def turn(n):
+            if n < PAIRS:
+                turn_and_quantise(x_rows[n], x_mx[n], interleaved=True)
+            else:
+                turn_and_quantise(a_rows[n - PAIRS], a_mx[n - PAIRS], interleaved=False)
+
+        for n in range(AHEAD):
+            turn(n)
+        for i in range(PAIRS):
+            project(i)
+            turn(i + AHEAD)
+            if i % 2 == 1:
+                quantise_h(i // 2)
+        for n in range(PAIRS + AHEAD, 2 * PAIRS):
+            turn(n)
+        for i in range(PAIRS):
+            aggregate(i)

@@ -22,6 +22,7 @@ PASSES = 2
 PAIRS = NODES // (2 * P)
 AHEAD = 2
 WORDS = K_PASS // 2
+EPS_COLUMNS = 32
 
 FLOPS = 2 * NODES * FEATURES * HIDDEN + 2 * NODES * NODES * HIDDEN
 
@@ -42,8 +43,9 @@ def tile_gin_pa_kernel(tc, X, A, W_in_words, W_in_scales, b_in, eps0, out):
         a_rows = [keep.tile([P, 2, NODES], BF16, name="a_rows%d" % i) for i in range(PAIRS)]
         w_codes = keep.tile([P, PASSES, PACK * HIDDEN], U8, name="w_codes", align_bytes=64)
         w_scales = keep.tile([P, PASSES, HIDDEN], U8, name="w_scales", align_bytes=64)
-        bias = keep.tile([P, HIDDEN], BF16, name="bias")
-        eps = keep.tile([P, 1], BF16, name="eps")
+        first_row = keep.tile([P, HIDDEN + EPS_COLUMNS], BF16, name="first_row")
+        ones = keep.tile([P, P], BF16, name="ones")
+        bias = keep.tile([P, HIDDEN], F32, name="bias")
         one_plus_eps = keep.tile([P, 1], F32, name="one_plus_eps")
         identity = keep.tile([P, P], F32, name="identity")
         h = [keep.tile([P, PACK, HIDDEN], F32, name="h%d" % g) for g in range(PASSES)]
@@ -67,8 +69,10 @@ def tile_gin_pa_kernel(tc, X, A, W_in_words, W_in_scales, b_in, eps0, out):
 
         nc.vector.memset(w_scales[:].rearrange("p g n -> p (g n)").bitcast(I32), 0)
         make_identity(nc, identity[:])
-        nc.gpsimd.dma_start(out=bias[:], in_=b_in.partition_broadcast(P))
-        nc.gpsimd.dma_start(out=eps[:], in_=eps0.partition_broadcast(P))
+        nc.vector.memset(first_row[:], 0.0)
+        nc.vector.memset(ones[:], 1.0)
+        nc.scalar.dma_start(out=first_row[0:1, 0:HIDDEN], in_=b_in.unsqueeze(0))
+        nc.scalar.dma_start(out=first_row[0:1, HIDDEN : HIDDEN + 1], in_=eps0.unsqueeze(0))
 
         nc.sync.dma_start(out=x_rows[0][:], in_=x_pairs[0])
         nc.sync.dma_start(out=x_rows[1][:], in_=x_pairs[1])
@@ -83,8 +87,6 @@ def tile_gin_pa_kernel(tc, X, A, W_in_words, W_in_scales, b_in, eps0, out):
             nc.sync.dma_start(out=x_rows[i][:], in_=x_pairs[i])
         for i in range(PAIRS):
             nc.sync.dma_start(out=a_rows[i][:], in_=a_pairs[i])
-
-        nc.vector.tensor_scalar_add(out=one_plus_eps[:], in0=eps[:], scalar1=1.0)
 
         def turn_and_quantise(rows, mx, interleaved):
             for e in range(2):
@@ -119,6 +121,11 @@ def tile_gin_pa_kernel(tc, X, A, W_in_words, W_in_scales, b_in, eps0, out):
                     start=(g == 0),
                     stop=(g == PASSES - 1),
                 )
+            return sums
+
+        def spread_first_row(columns, width):
+            sums = sum_banks.tile([P, HIDDEN], F32)
+            nc.tensor.matmul(out=sums[:, 0:width], lhsT=ones[:], rhs=first_row[:, columns], start=True, stop=True)
             return sums
 
         def project(i):
@@ -170,6 +177,10 @@ def tile_gin_pa_kernel(tc, X, A, W_in_words, W_in_scales, b_in, eps0, out):
             else:
                 turn_and_quantise(a_rows[n - PAIRS], a_mx[n - PAIRS], interleaved=False)
 
+        sums = spread_first_row(slice(0, HIDDEN), HIDDEN)
+        nc.scalar.copy(out=bias[:], in_=sums[:])
+        sums = spread_first_row(slice(HIDDEN, HIDDEN + EPS_COLUMNS), EPS_COLUMNS)
+        nc.vector.tensor_scalar_add(out=one_plus_eps[:], in0=sums[:, 0:1], scalar1=1.0)
         for n in range(AHEAD):
             turn(n)
         for i in range(PAIRS):

@@ -35,8 +35,7 @@ def tile_gin_pa_kernel(tc, X, A, W_in_words, W_in_scales, b_in, eps0, out):
 
     with ExitStack() as ctx:
         keep = ctx.enter_context(tc.tile_pool(name="keep", bufs=1))
-        turned_banks = ctx.enter_context(tc.psum_pool(name="turned_banks", bufs=4))
-        sum_banks = ctx.enter_context(tc.psum_pool(name="sum_banks", bufs=4))
+        banks = ctx.enter_context(tc.psum_pool(name="banks", bufs=8))
         ctx.enter_context(tc.manual_schedule())
 
         x_rows = [keep.tile([P, 2, FEATURES], BF16, name="x_rows%d" % i) for i in range(PAIRS)]
@@ -74,7 +73,8 @@ def tile_gin_pa_kernel(tc, X, A, W_in_words, W_in_scales, b_in, eps0, out):
         nc.scalar.dma_start(out=first_row[0:1, 0:HIDDEN], in_=b_in.unsqueeze(0))
         nc.scalar.dma_start(out=first_row[0:1, HIDDEN : HIDDEN + 1], in_=eps0.unsqueeze(0))
 
-        nc.sync.dma_start(out=x_rows[0][:], in_=x_pairs[0])
+        for e in range(2):
+            nc.sync.dma_start(out=x_rows[0][:, e, :], in_=x_pairs[0][:, e, :])
         nc.sync.dma_start(out=x_rows[1][:], in_=x_pairs[1])
         scale_rows = W_in_scales.rearrange("g (q r) n -> r q g n", r=4)
         for r in range(4):
@@ -88,10 +88,10 @@ def tile_gin_pa_kernel(tc, X, A, W_in_words, W_in_scales, b_in, eps0, out):
         for i in range(PAIRS):
             nc.sync.dma_start(out=a_rows[i][:], in_=a_pairs[i])
 
-        def turn_and_quantise(rows, mx, interleaved):
+        def turn(rows, mx, interleaved):
             for e in range(2):
                 words = rows[:, e, :].bitcast(F32)
-                turned = turned_banks.tile([P, PASSES, 2, P], F32)
+                turned = banks.tile([P, PASSES, 2, P], F32, tag="bank")
                 for g in range(PASSES):
                     for u in range(2):
                         if interleaved:
@@ -103,6 +103,8 @@ def tile_gin_pa_kernel(tc, X, A, W_in_words, W_in_scales, b_in, eps0, out):
                     out=mx["grouped"][:, e].bitcast(F32),
                     in_=turned[:].rearrange("p g u n -> p g n u"),
                 )
+
+        def quantise(mx):
             nc.vector.quantize_mx(
                 out=mx["codes"][:].rearrange("p e g n -> p (e g n)").bitcast(FP8X4),
                 scales=mx["scales"][:].rearrange("p e g n -> p (e g n)"),
@@ -110,7 +112,7 @@ def tile_gin_pa_kernel(tc, X, A, W_in_words, W_in_scales, b_in, eps0, out):
             )
 
         def multiply(mx, e, moving_codes, moving_scales):
-            sums = sum_banks.tile([P, HIDDEN], F32)
+            sums = banks.tile([P, HIDDEN], F32, tag="bank")
             for g in range(PASSES):
                 nc.tensor.matmul_mx(
                     out=sums[:],
@@ -124,7 +126,7 @@ def tile_gin_pa_kernel(tc, X, A, W_in_words, W_in_scales, b_in, eps0, out):
             return sums
 
         def spread_first_row(columns, width):
-            sums = sum_banks.tile([P, HIDDEN], F32)
+            sums = banks.tile([P, HIDDEN], F32, tag="bank")
             nc.tensor.matmul(out=sums[:, 0:width], lhsT=ones[:], rhs=first_row[:, columns], start=True, stop=True)
             return sums
 
@@ -139,13 +141,15 @@ def tile_gin_pa_kernel(tc, X, A, W_in_words, W_in_scales, b_in, eps0, out):
                 j = 2 * i + e
                 nc.vector.tensor_tensor(out=h[j // PACK][:, j % PACK, :], in0=sums[:], in1=bias[:], op=ADD)
 
+        def regroup_h(g, vector_columns):
+            grouped = h_grouped[g][:].rearrange("p (c i) t -> p c t i", i=4)
+            tiles = h[g][:].rearrange("p t (c i) -> p c t i", i=4)
+            split = vector_columns // 4
+            if split > 0:
+                nc.vector.tensor_copy(out=grouped[:, 0:split], in_=tiles[:, 0:split])
+            nc.scalar.copy(out=grouped[:, split:], in_=tiles[:, split:])
+
         def quantise_h(g):
-            half = HIDDEN // 2
-            for copy, columns in ((nc.vector.tensor_copy, slice(0, half)), (nc.scalar.copy, slice(half, HIDDEN))):
-                copy(
-                    out=h_grouped[g][:, columns, :].rearrange("p (c i) t -> p c t i", i=4),
-                    in_=h[g][:, :, columns].rearrange("p t (c i) -> p c t i", i=4),
-                )
             nc.vector.quantize_mx(
                 out=h_codes[g][:].bitcast(FP8X4),
                 scales=h_scales[g][:],
@@ -171,24 +175,35 @@ def tile_gin_pa_kernel(tc, X, A, W_in_words, W_in_scales, b_in, eps0, out):
                 )
                 nc.sync.dma_start(out=out_pairs[i][:, e, :], in_=result[i][:, e, :])
 
-        def turn(n):
-            if n < PAIRS:
-                turn_and_quantise(x_rows[n], x_mx[n], interleaved=True)
-            else:
-                turn_and_quantise(a_rows[n - PAIRS], a_mx[n - PAIRS], interleaved=False)
+        def prepare_x(i):
+            turn(x_rows[i], x_mx[i], interleaved=True)
+            quantise(x_mx[i])
 
+        def turn_a(i):
+            turn(a_rows[i], a_mx[i], interleaved=False)
+
+        for i in range(AHEAD):
+            prepare_x(i)
         sums = spread_first_row(slice(0, HIDDEN), HIDDEN)
         nc.scalar.copy(out=bias[:], in_=sums[:])
         sums = spread_first_row(slice(HIDDEN, HIDDEN + EPS_COLUMNS), EPS_COLUMNS)
         nc.vector.tensor_scalar_add(out=one_plus_eps[:], in0=sums[:, 0:1], scalar1=1.0)
-        for n in range(AHEAD):
-            turn(n)
-        for i in range(PAIRS):
+
+        for i in range(AHEAD):
             project(i)
-            turn(i + AHEAD)
-            if i % 2 == 1:
-                quantise_h(i // 2)
-        for n in range(PAIRS + AHEAD, 2 * PAIRS):
-            turn(n)
+            prepare_x(i + AHEAD)
+        regroup_h(0, vector_columns=0)
+        project(2)
+        turn_a(0)
+        project(3)
+        regroup_h(1, vector_columns=HIDDEN // 2)
+        for i in range(1, PAIRS):
+            turn_a(i)
+        quantise_h(0)
+        quantise(a_mx[0])
+        quantise_h(1)
+        quantise(a_mx[1])
         for i in range(PAIRS):
             aggregate(i)
+            if i + AHEAD < PAIRS:
+                quantise(a_mx[i + AHEAD])

@@ -182,12 +182,12 @@ def tile_gin_pa_kernel(tc, X, A, W_in_words, W_in_scales, b_in, eps0, out):
         def turn_a(i):
             turn(a_rows[i], a_mx[i], interleaved=False)
 
-        for i in range(AHEAD):
-            prepare_x(i)
+        prepare_x(0)
         sums = spread_first_row(slice(0, HIDDEN), HIDDEN)
         nc.scalar.copy(out=bias[:], in_=sums[:])
         sums = spread_first_row(slice(HIDDEN, HIDDEN + EPS_COLUMNS), EPS_COLUMNS)
         nc.vector.tensor_scalar_add(out=one_plus_eps[:], in0=sums[:, 0:1], scalar1=1.0)
+        prepare_x(1)
 
         for i in range(AHEAD):
             project(i)

@@ -66,6 +66,14 @@ def tile_gin_pa_kernel(tc, X, A, W_in_words, W_in_scales, b_in, eps0, out):
         x_mx = [quantised_pair("x%d" % i) for i in range(PAIRS)]
         a_mx = [quantised_pair("a%d" % i) for i in range(PAIRS)]
 
+        warm = keep.tile([P, HIDDEN], BF16, name="warm")
+        nc.vector.memset(warm[:], 0.0)
+        idle = banks.tile([P, HIDDEN], F32, tag="bank")
+
+        def warm_up(count):
+            for i in range(count):
+                nc.tensor.matmul(out=idle[:], lhsT=warm[:, 0:P], rhs=warm[:], start=True, stop=True)
+
         nc.vector.memset(w_scales[:].rearrange("p g n -> p (g n)").bitcast(I32), 0)
         make_identity(nc, identity[:])
         nc.vector.memset(first_row[:], 0.0)
@@ -182,7 +190,9 @@ def tile_gin_pa_kernel(tc, X, A, W_in_words, W_in_scales, b_in, eps0, out):
         def turn_a(i):
             turn(a_rows[i], a_mx[i], interleaved=False)
 
+        warm_up(5)
         prepare_x(0)
+        warm_up(1)
         sums = spread_first_row(slice(0, HIDDEN), HIDDEN)
         nc.scalar.copy(out=bias[:], in_=sums[:])
         sums = spread_first_row(slice(HIDDEN, HIDDEN + EPS_COLUMNS), EPS_COLUMNS)

@@ -67,17 +67,17 @@ def tile_gin_pa_kernel(tc, X, A, W_in_words, W_in_scales, b_in, eps0, out):
         a_mx = [quantised_pair("a%d" % i) for i in range(PAIRS)]
 
         warm = keep.tile([P, HIDDEN], BF16, name="warm")
-        nc.vector.memset(warm[:], 0.0)
-        idle = banks.tile([P, HIDDEN], F32, tag="bank")
+        nc.vector.memset(warm[:].bitcast(I32), 0)
 
         def warm_up(count):
+            idle = banks.tile([P, HIDDEN], F32, tag="bank")
             for i in range(count):
                 nc.tensor.matmul(out=idle[:], lhsT=warm[:, 0:P], rhs=warm[:], start=True, stop=True)
 
         nc.vector.memset(w_scales[:].rearrange("p g n -> p (g n)").bitcast(I32), 0)
         make_identity(nc, identity[:])
-        nc.vector.memset(first_row[:], 0.0)
-        nc.vector.memset(ones[:], 1.0)
+        nc.vector.memset(first_row[:].bitcast(I32), 0)
+        nc.gpsimd.memset(ones[:], 1.0)
         nc.scalar.dma_start(out=first_row[0:1, 0:HIDDEN], in_=b_in.unsqueeze(0))
         nc.scalar.dma_start(out=first_row[0:1, HIDDEN : HIDDEN + 1], in_=eps0.unsqueeze(0))
 
@@ -190,7 +190,7 @@ def tile_gin_pa_kernel(tc, X, A, W_in_words, W_in_scales, b_in, eps0, out):
         def turn_a(i):
             turn(a_rows[i], a_mx[i], interleaved=False)
 
-        warm_up(5)
+        warm_up(4)
         prepare_x(0)
         warm_up(1)
         sums = spread_first_row(slice(0, HIDDEN), HIDDEN)
@@ -209,6 +209,8 @@ def tile_gin_pa_kernel(tc, X, A, W_in_words, W_in_scales, b_in, eps0, out):
         regroup_h(1, vector_columns=HIDDEN // 2)
         for i in range(1, PAIRS):
             turn_a(i)
+            if i > 1:
+                warm_up(2)
         quantise_h(0)
         quantise(a_mx[0])
         quantise_h(1)

@@ -40,8 +40,8 @@ def tile_gin_pa_kernel(tc, X, A, W_in_words, W_in_scales, b_in, eps0, out):
 
         x_rows = [keep.tile([P, 2, FEATURES], BF16, name="x_rows%d" % i) for i in range(PAIRS)]
         a_rows = [keep.tile([P, 2, NODES], BF16, name="a_rows%d" % i) for i in range(PAIRS)]
-        w_codes = keep.tile([P, PASSES, PACK * HIDDEN], U8, name="w_codes", align_bytes=64)
-        w_scales = keep.tile([P, PASSES, HIDDEN], U8, name="w_scales", align_bytes=64)
+        w_codes = keep.tile([P, PASSES, PACK * HIDDEN], U8, name="w_codes", align_bytes=256)
+        w_scales = keep.tile([P, PASSES, HIDDEN], U8, name="w_scales", align_bytes=256)
         first_row = keep.tile([P, HIDDEN + EPS_COLUMNS], BF16, name="first_row")
         ones = keep.tile([P, P], BF16, name="ones")
         bias = keep.tile([P, HIDDEN], F32, name="bias")
@@ -49,18 +49,18 @@ def tile_gin_pa_kernel(tc, X, A, W_in_words, W_in_scales, b_in, eps0, out):
         identity = keep.tile([P, P], F32, name="identity")
         h = [keep.tile([P, PACK, HIDDEN], F32, name="h%d" % g) for g in range(PASSES)]
         h_grouped = [
-            keep.tile([P, HIDDEN, PACK], BF16, name="h_grouped%d" % g, align_bytes=64)
+            keep.tile([P, HIDDEN, PACK], BF16, name="h_grouped%d" % g, align_bytes=256)
             for g in range(PASSES)
         ]
-        h_codes = [keep.tile([P, HIDDEN], U32, name="h_codes%d" % g, align_bytes=64) for g in range(PASSES)]
-        h_scales = [keep.tile([P, HIDDEN], U8, name="h_scales%d" % g, align_bytes=64) for g in range(PASSES)]
+        h_codes = [keep.tile([P, HIDDEN], U32, name="h_codes%d" % g, align_bytes=256) for g in range(PASSES)]
+        h_scales = [keep.tile([P, HIDDEN], U8, name="h_scales%d" % g, align_bytes=256) for g in range(PASSES)]
         result = [keep.tile([P, 2, HIDDEN], F32, name="result%d" % i) for i in range(PAIRS)]
 
         def quantised_pair(name):
             return {
-                "grouped": keep.tile([P, 2, PASSES, P, PACK], BF16, name=name + "_grouped", align_bytes=64),
-                "codes": keep.tile([P, 2, PASSES, P], U32, name=name + "_codes", align_bytes=64),
-                "scales": keep.tile([P, 2, PASSES, P], U8, name=name + "_scales", align_bytes=64),
+                "grouped": keep.tile([P, 2, PASSES, P, PACK], BF16, name=name + "_grouped", align_bytes=256),
+                "codes": keep.tile([P, 2, PASSES, P], U32, name=name + "_codes", align_bytes=256),
+                "scales": keep.tile([P, 2, PASSES, P], U8, name=name + "_scales", align_bytes=256),
             }
 
         x_mx = [quantised_pair("x%d" % i) for i in range(PAIRS)]

from contextlib import ExitStack

import concourse.mybir as mybir
from concourse.masks import make_identity

F32 = mybir.dt.float32
BF16 = mybir.dt.bfloat16
I32 = mybir.dt.int32
U32 = mybir.dt.uint32
U8 = mybir.dt.uint8
FP8X4 = mybir.dt.float8_e4m3fn_x4
ADD = mybir.AluOpType.add
MULT = mybir.AluOpType.mult

P = 128
PACK = 4
K_PASS = P * PACK
NODES = 1024
FEATURES = 1024
HIDDEN = 512
PASSES = 2
PAIRS = NODES // (2 * P)
AHEAD = 2
WORDS = K_PASS // 2
EPS_COLUMNS = 32

FLOPS = 2 * NODES * FEATURES * HIDDEN + 2 * NODES * NODES * HIDDEN


def tile_gin_pa_kernel(tc, X, A, W_in_words, W_in_scales, b_in, eps0, out):
    nc = tc.nc
    x_pairs = X.rearrange("(i p e) k -> i p e k", p=P, e=2)
    a_pairs = A.rearrange("(i p e) k -> i p e k", p=P, e=2)
    out_pairs = out.rearrange("(i p e) f -> i p e f", p=P, e=2)

    with ExitStack() as ctx:
        keep = ctx.enter_context(tc.tile_pool(name="keep", bufs=1))
        banks = ctx.enter_context(tc.psum_pool(name="banks", bufs=8))
        ctx.enter_context(tc.manual_schedule())

        x_rows = [keep.tile([P, 2, FEATURES], BF16, name="x_rows%d" % i) for i in range(PAIRS)]
        a_rows = [keep.tile([P, 2, NODES], BF16, name="a_rows%d" % i) for i in range(PAIRS)]
        w_codes = keep.tile([P, PASSES, PACK * HIDDEN], U8, name="w_codes", align_bytes=256)
        w_scales = keep.tile([P, PASSES, HIDDEN], U8, name="w_scales", align_bytes=256)
        first_row = keep.tile([P, HIDDEN + EPS_COLUMNS], BF16, name="first_row")
        ones = keep.tile([P, P], BF16, name="ones")
        bias = keep.tile([P, HIDDEN], F32, name="bias")
        one_plus_eps = keep.tile([P, 1], F32, name="one_plus_eps")
        identity = keep.tile([P, P], F32, name="identity")
        h = [keep.tile([P, PACK, HIDDEN], F32, name="h%d" % g) for g in range(PASSES)]
        h_grouped = [
            keep.tile([P, HIDDEN, PACK], BF16, name="h_grouped%d" % g, align_bytes=256)
            for g in range(PASSES)
        ]
        h_codes = [keep.tile([P, HIDDEN], U32, name="h_codes%d" % g, align_bytes=256) for g in range(PASSES)]
        h_scales = [keep.tile([P, HIDDEN], U8, name="h_scales%d" % g, align_bytes=256) for g in range(PASSES)]
        result = [keep.tile([P, 2, HIDDEN], F32, name="result%d" % i) for i in range(PAIRS)]

        def quantised_pair(name):
            return {
                "grouped": keep.tile([P, 2, PASSES, P, PACK], BF16, name=name + "_grouped", align_bytes=256),
                "codes": keep.tile([P, 2, PASSES, P], U32, name=name + "_codes", align_bytes=256),
                "scales": keep.tile([P, 2, PASSES, P], U8, name=name + "_scales", align_bytes=256),
            }

        x_mx = [quantised_pair("x%d" % i) for i in range(PAIRS)]
        a_mx = [quantised_pair("a%d" % i) for i in range(PAIRS)]

        warm = keep.tile([P, HIDDEN], BF16, name="warm")
        nc.vector.memset(warm[:].bitcast(I32), 0)

        def warm_up(count):
            idle = banks.tile([P, HIDDEN], F32, tag="bank")
            for i in range(count):
                nc.tensor.matmul(out=idle[:], lhsT=warm[:, 0:P], rhs=warm[:], start=True, stop=True)

        nc.vector.memset(w_scales[:].rearrange("p g n -> p (g n)").bitcast(I32), 0)
        make_identity(nc, identity[:])
        nc.vector.memset(first_row[:].bitcast(I32), 0)
        nc.gpsimd.memset(ones[:], 1.0)
        nc.scalar.dma_start(out=first_row[0:1, 0:HIDDEN], in_=b_in.unsqueeze(0))
        nc.scalar.dma_start(out=first_row[0:1, HIDDEN : HIDDEN + 1], in_=eps0.unsqueeze(0))

        for e in range(2):
            nc.sync.dma_start(out=x_rows[0][:, e, :], in_=x_pairs[0][:, e, :])
        nc.sync.dma_start(out=x_rows[1][:], in_=x_pairs[1])
        scale_rows = W_in_scales.rearrange("g (q r) n -> r q g n", r=4)
        for r in range(4):
            nc.sync.dma_start(out=w_scales[r:P:32].bitcast(I32), in_=scale_rows[r].bitcast(I32))
        nc.sync.dma_start(
            out=w_codes[:].bitcast(I32),
            in_=W_in_words.rearrange("g p n t -> p g (n t)").bitcast(I32),
        )
        for i in range(AHEAD, PAIRS):
            nc.sync.dma_start(out=x_rows[i][:], in_=x_pairs[i])
        for i in range(PAIRS):
            nc.sync.dma_start(out=a_rows[i][:], in_=a_pairs[i])

        def turn(rows, mx, interleaved):
            for e in range(2):
                words = rows[:, e, :].bitcast(F32)
                turned = banks.tile([P, PASSES, 2, P], F32, tag="bank")
                for g in range(PASSES):
                    for u in range(2):
                        if interleaved:
                            columns = words[:, WORDS * g + u : WORDS * (g + 1) : 2]
                        else:
                            columns = words[:, WORDS * g + P * u : WORDS * g + P * (u + 1)]
                        nc.tensor.transpose(turned[:, g, u, :], columns, identity[:])
                nc.scalar.copy(
                    out=mx["grouped"][:, e].bitcast(F32),
                    in_=turned[:].rearrange("p g u n -> p g n u"),
                )

        def quantise(mx):
            nc.vector.quantize_mx(
                out=mx["codes"][:].rearrange("p e g n -> p (e g n)").bitcast(FP8X4),
                scales=mx["scales"][:].rearrange("p e g n -> p (e g n)"),
                in_=mx["grouped"][:].rearrange("p e g n t -> p (e g n t)"),
            )

        def multiply(mx, e, moving_codes, moving_scales):
            sums = banks.tile([P, HIDDEN], F32, tag="bank")
            for g in range(PASSES):
                nc.tensor.matmul_mx(
                    out=sums[:],
                    lhsT=mx["codes"][:, e, g, :].bitcast(FP8X4),
                    lhsT_scale=mx["scales"][:, e, g, :],
                    rhs=moving_codes[g],
                    rhs_scale=moving_scales[g],
                    start=(g == 0),
                    stop=(g == PASSES - 1),
                )
            return sums

        def spread_first_row(columns, width):
            sums = banks.tile([P, HIDDEN], F32, tag="bank")
            nc.tensor.matmul(out=sums[:, 0:width], lhsT=ones[:], rhs=first_row[:, columns], start=True, stop=True)
            return sums

        def project(i):
            for e in range(2):
                sums = multiply(
                    x_mx[i],
                    e,
                    [w_codes[:, g, :].bitcast(FP8X4) for g in range(PASSES)],
                    [w_scales[:, g, :] for g in range(PASSES)],
                )
                j = 2 * i + e
                nc.vector.tensor_tensor(out=h[j // PACK][:, j % PACK, :], in0=sums[:], in1=bias[:], op=ADD)

        def regroup_h(g, vector_columns):
            grouped = h_grouped[g][:].rearrange("p (c i) t -> p c t i", i=4)
            tiles = h[g][:].rearrange("p t (c i) -> p c t i", i=4)
            split = vector_columns // 4
            if split > 0:
                nc.vector.tensor_copy(out=grouped[:, 0:split], in_=tiles[:, 0:split])
            nc.scalar.copy(out=grouped[:, split:], in_=tiles[:, split:])

        def quantise_h(g):
            nc.vector.quantize_mx(
                out=h_codes[g][:].bitcast(FP8X4),
                scales=h_scales[g][:],
                in_=h_grouped[g][:].rearrange("p f t -> p (f t)"),
            )

        def aggregate(i):
            for e in range(2):
                sums = multiply(
                    a_mx[i],
                    e,
                    [h_codes[g][:].bitcast(FP8X4) for g in range(PASSES)],
                    [h_scales[g][:] for g in range(PASSES)],
                )
                j = 2 * i + e
                nc.vector.scalar_tensor_tensor(
                    out=result[i][:, e, :],
                    in0=h[j // PACK][:, j % PACK, :],
                    scalar=one_plus_eps[:, 0:1],
                    in1=sums[:],
                    op0=MULT,
                    op1=ADD,
                )
                nc.sync.dma_start(out=out_pairs[i][:, e, :], in_=result[i][:, e, :])

        def prepare_x(i):
            turn(x_rows[i], x_mx[i], interleaved=True)
            quantise(x_mx[i])

        def turn_a(i):
            turn(a_rows[i], a_mx[i], interleaved=False)

        warm_up(4)
        prepare_x(0)
        warm_up(1)
        sums = spread_first_row(slice(0, HIDDEN), HIDDEN)
        nc.scalar.copy(out=bias[:], in_=sums[:])
        sums = spread_first_row(slice(HIDDEN, HIDDEN + EPS_COLUMNS), EPS_COLUMNS)
        nc.vector.tensor_scalar_add(out=one_plus_eps[:], in0=sums[:, 0:1], scalar1=1.0)
        prepare_x(1)

        for i in range(AHEAD):
            project(i)
            prepare_x(i + AHEAD)
        regroup_h(0, vector_columns=0)
        project(2)
        turn_a(0)
        project(3)
        regroup_h(1, vector_columns=HIDDEN // 2)
        for i in range(1, PAIRS):
            turn_a(i)
            if i > 1:
                warm_up(2)
        quantise_h(0)
        quantise(a_mx[0])
        quantise_h(1)
        quantise(a_mx[1])
        for i in range(PAIRS):
            aggregate(i)
            if i + AHEAD < PAIRS:
                quantise(a_mx[i + AHEAD])
